import numpy as np
import ml_dtypes


def mxq(x, axis, fmt="e4m3"):
    dtype, down = {"e4m3": (ml_dtypes.float8_e4m3fn, 7), "e5m2": (ml_dtypes.float8_e5m2, 14)}[fmt]
    v = np.moveaxis(np.asarray(x, np.float32).astype(ml_dtypes.bfloat16).astype(np.float64), axis, -1)
    blocks = v.reshape(v.shape[:-1] + (-1, 32))
    amax = np.abs(blocks).max(-1, keepdims=True)
    byte = np.maximum(np.where(amax > 0, np.frexp(amax)[1] - 1 + 127, 0) - down, 1)
    scale = np.exp2(byte - 127.0)
    codes = (blocks / scale).astype(np.float32).astype(dtype).astype(np.float64)
    return np.moveaxis((codes * scale).reshape(v.shape), -1, axis)


WIDE = False


def mx_kscale(k):
    if not WIDE:
        return np.ones(k)
    levels = np.array([30, -30])
    if k % 512:
        return np.exp2(np.random.permutation(np.resize(levels, k // 32))).repeat(32)
    a = np.empty((k // 512, 16))
    for p in range(k // 512):
        a[p, :8] = np.random.permutation(np.resize(levels, 8))
        for g in range(8):
            far = levels[np.abs(levels - a[p, g]) >= 10]
            a[p, g + 8] = far[np.random.randint(len(far))]
    return np.exp2(a.ravel()).repeat(32)


BF16 = ml_dtypes.bfloat16


def bf(x):
    return np.asarray(x, np.float32).astype(BF16)


def f64(x):
    return np.asarray(x).astype(np.float64)


N, L, H, E, HEADS, R = 512, 4, 512, 512, 6, 4
EPS = 1e-12


def l2norm(v):
    n = np.sqrt((v * v).sum(-1, keepdims=True))
    return v / np.maximum(n, EPS)


def setup_inputs():
    s = mx_kscale(H)
    gloss = np.random.standard_normal((N, 1, H))
    amp_w = 0.5 + np.random.random_sample((N, L, 1))
    amp_s = 0.5 + np.random.random_sample((N, 1))
    feature = amp_w * 0.7 * (gloss + np.random.standard_normal((N, L, H)))
    aspect_v = amp_s * np.random.standard_normal((N, H))
    return {"feature": bf(feature * s), "aspect_v": bf(aspect_v * s),
            "W": bf(np.random.standard_normal((HEADS, E, H)) / np.sqrt(H) / s),
            "b": bf(0.2 * np.random.standard_normal((HEADS, E)))}


def reference(feature, aspect_v, W, b):
    wt = mxq(f64(W).transpose(0, 2, 1), 1, "e4m3")
    bias = f64(b)
    q = (mxq(f64(aspect_v), 1, "e5m2") @ wt) + bias[:, None, :]
    fh = (mxq(f64(feature), 2, "e5m2").reshape(N * L, H) @ wt).reshape(HEADS, N, L, E) + bias[:, None, None, :]
    return l2norm(q), l2norm(fh).mean(axis=2)

@@ -1,0 +1,290 @@
+from contextlib import ExitStack
+
+import concourse.mybir as mybir
+from concourse.masks import make_identity
+
+N, L, H, E, HEADS = 512, 4, 512, 512, 6
+EPS = 1e-12
+FLOPS = 2 * HEADS * N * (L + 1) * H * E
+
+F32 = mybir.dt.float32
+BF16 = mybir.dt.bfloat16
+U32 = mybir.dt.uint32
+U8 = mybir.dt.uint8
+E4M3X4 = mybir.dt.float8_e4m3fn_x4
+E5M2X4 = mybir.dt.float8_e5m2_x4
+ALU = mybir.AluOpType
+ACT = mybir.ActivationFunctionType
+AX = mybir.AxisListType
+
+P = 128
+Q = 4
+POOL_PASSES = (0, 8)
+N_POOL = 11
+SCALAR_Q = 1
+V_COPY_STEPS = 4
+FIRST = 2
+LAG = 2
+SHARE_AT = 1
+VC = 1
+C_AT = 0
+I_AT = 1
+SENSES = (4, 8, 11, 14, 15, 16)
+
+
+def tile_biencodermodel_pa_kernel(tc, feature, aspect_v, W, b, out_0, out_1):
+    nc = tc.nc
+    with ExitStack() as ctx:
+        keep = ctx.enter_context(tc.tile_pool(name="keep", bufs=1))
+        work = ctx.enter_context(tc.tile_pool(name="work", bufs=2))
+        psum = ctx.enter_context(tc.psum_pool(name="psum", bufs=1))
+        ctx.enter_context(tc.manual_schedule())
+
+        units = [("W", 0), ("F", 0), ("F", 1), ("W", 1), ("F", None), ("F", 2), ("W", 2), ("F", 3), ("W", 3), ("W", 4), ("W", 5)]
+        sources = {("W", h): W[h].rearrange("(c p) k -> p c k", p=P) for h in range(HEADS)}
+        sources.update({("F", j): feature[j * P : (j + 1) * P] for j in range(Q)})
+        sources[("F", None)] = aspect_v.rearrange("(j p) k -> p j k", p=P)
+        means = sorted(
+            [(j, h) for j in range(Q) for h in range(HEADS)], key=lambda g: max(units.index(("F", g[0])), units.index(("W", g[1])))
+        )
+        n_steps = N_POOL + HEADS
+        senses = list(SENSES)
+        once, twice = [], []
+        for t in range(n_steps):
+            once.append((None, senses.index(t)) if t in senses else means.pop(0))
+            if t >= FIRST and len(twice) < Q * HEADS - N_POOL:
+                twice.append(means.pop(0))
+        ready = {-1: units[2:3], 0: units[3:5], 1: units[5:7]}
+        ready.update({t: units[t + 5 : t + 6] for t in range(2, n_steps + 1)})
+
+        bias_rows = keep.tile([P, P], BF16, name="bias_rows")
+        nc.vector.memset(bias_rows[:], 0.0)
+        nc.scalar.dma_start(out=bias_rows[0 : HEADS * Q, :], in_=b.rearrange("h (c p) -> (h c) p", p=P))
+        raw, bias_all = {}, {}
+        for key in units:
+            raw[key] = keep.tile([P, Q, H], BF16, name="raw_%s%s" % key)
+            nc.sync.dma_start(out=raw[key][:], in_=sources[key])
+            if key == ("F", 0) or (key[0] == "W" and key[1] > 0):
+                h = key[1]
+                bias_all[h] = keep.tile([P, E], BF16, name="bias_all%d" % h)
+                nc.sync.dma_start(out=bias_all[h][:], in_=b[h].partition_broadcast(P))
+
+        ident = keep.tile([P, P], F32, name="ident")
+        make_identity(nc, ident[:])
+        ident_bf = keep.tile([P, P], BF16, name="ident_bf")
+        make_identity(nc, ident_bf[:])
+        bias_col = keep.tile([P, HEADS * Q], F32, name="bias_col")
+
+        codes, scales, grouped, turned = {}, {}, {}, {}
+
+        def turn(key, half):
+            if half == 0:
+                grouped[key] = work.tile([P, Q * P * 4], BF16, name="grouped", align_bytes=64, bufs=4)
+            bank = psum.tile([P, 2, 2, P], F32, name="bank", bufs=8)
+            for i in range(2):
+                words = raw[key][:, 2 * half + i, :].bitcast(F32)
+                for u in range(2):
+                    nc.tensor.transpose(bank[:, i, u, :], words[:, u::2], ident[:])
+            dst = grouped[key][:].bitcast(F32).rearrange("p (i r u) -> p i r u", i=Q, u=2)
+            turned[key, half] = dst[:, 2 * half : 2 * half + 2], bank[:].rearrange("p i u r -> p i r u")
+
+        def quantise(key):
+            codes[key] = keep.tile([P, Q * P], U32, name="codes_%s%s" % key, align_bytes=64)
+            scales[key] = keep.tile([P, Q * P], U8, name="scales_%s%s" % key, align_bytes=64)
+            nc.vector.quantize_mx(
+                out=codes[key][:].bitcast(E4M3X4 if key[0] == "W" else E5M2X4), scales=scales[key][:], in_=grouped[key][:]
+            )
+
+        def product(stat, i, mov):
+            bank = psum.tile([P, E], F32, name="bank", bufs=8)
+            cols = slice(i * P, (i + 1) * P)
+            nc.tensor.matmul_mx(
+                out=bank[:],
+                lhsT=codes[stat][:, cols].bitcast(E4M3X4 if stat[0] == "W" else E5M2X4),
+                lhsT_scale=scales[stat][:, cols],
+                rhs=codes[mov][:].bitcast(E4M3X4 if mov[0] == "W" else E5M2X4),
+                rhs_scale=scales[mov][:],
+                start=True,
+                stop=True,
+            )
+            return bank
+
+        banks, squares, sumsq, ys, quarters, accs, sums, small = {}, {}, {}, {}, {}, {}, {}, {}
+        backlog, totals = [], {}
+
+        def copy_half(key, half, on_vector):
+            dst, src = turned[key, half]
+            if on_vector:
+                nc.vector.tensor_copy(out=dst, in_=src)
+            else:
+                nc.scalar.copy(out=dst, in_=src)
+
+        def bias_columns():
+            bank = psum.tile([P, P], BF16, name="bank", bufs=8)
+            nc.tensor.transpose(bank[:], bias_rows[:], ident_bf[:])
+            nc.vector.tensor_copy(out=bias_col[:], in_=bank[:, 0 : HEADS * Q])
+
+        def mm(name, stat, i, mov):
+            banks[name] = product(stat, i, mov)
+
+        def stats(t):
+            if t not in sumsq:
+                sumsq[t] = work.tile([P, 2 * Q], F32, name="sumsq", bufs=3)
+            return sumsq[t]
+
+        def add_bias(t, i):
+            if i == 0:
+                ys[t] = work.tile([P, Q, E], F32, name="y", bufs=6)
+            nc.vector.tensor_tensor(out=ys[t][:, i, :], in0=banks["p", t, i][:], in1=bias_all[once[t][1]][:], op=ALU.add)
+
+        def row_squares(t, i):
+            unread = work.tile([P, E], BF16, name="unread")
+            nc.scalar.activation(out=unread[:], in_=ys[t][:, i, :], func=ACT.Square, accum_out=stats(t)[:, i : i + 1])
+
+        def turned_squares(n, i):
+            if i == 0:
+                squares[n] = work.tile([P, Q, E], F32, name="squares")
+            col = Q * twice[n][1] + i
+            nc.scalar.activation(out=squares[n][:, i, :], in_=banks["f", n, i][:], func=ACT.Square, bias=bias_col[:, col : col + 1])
+
+        def fold(n, words):
+            if words[0] == 0:
+                sums[n] = psum.tile([P, Q, P], F32, name="bank", bufs=8)
+            for l in words:
+                for c in range(Q):
+                    nc.tensor.matmul(
+                        out=sums[n][:, l, :],
+                        lhsT=squares[n][:, c, l * P : (l + 1) * P],
+                        rhs=ident[:],
+                        start=(c == 0),
+                        stop=(c == Q - 1),
+                        is_transpose=True,
+                    )
+
+        def fold_sum(n, t):
+            nc.vector.tensor_reduce(out=stats(t)[:, Q:], in_=sums[n][:], axis=AX.X, op=ALU.add)
+
+        def clamp(t, cols):
+            small[t] = work.tile([P, 2 * Q], F32, name="excess")
+            nc.scalar.activation(out=small[t][:, cols], in_=sumsq[t][:, cols], func=ACT.Relu, bias=-EPS * EPS)
+
+        def root(t, cols):
+            norms = work.tile([P, 2 * Q], F32, name="norms")
+            parts = [(cols, 16.0)]
+            if t in senses:
+                parts = [(slice(0, Q), 1.0)] + ([(slice(Q, 2 * Q), 16.0)] if cols.stop > Q else [])
+            for part, factor in parts:
+                nc.scalar.activation(out=norms[:, part], in_=small[t][:, part], func=ACT.Sqrt, scale=factor, bias=factor * EPS * EPS)
+            small[t] = norms
+
+        def invert(t, cols):
+            quarters[t] = work.tile([P, 2 * Q], F32, name="quarter", bufs=8)
+            nc.vector.reciprocal(out=quarters[t][:, cols], in_=small[t][:, cols])
+            j, h = once[t]
+            if t in senses[HEADS - SCALAR_Q :]:
+                return
+            backlog.extend([(1, pool_scale, (t, i)) for i in range(Q)])
+            if j is not None:
+                backlog.extend([(2, pool_add, (t, i, k)) for i, k in ((0, 1), (2, 3), (0, 2))])
+
+        def scalar_scale(t, i, on_vector):
+            if on_vector:
+                nc.vector.tensor_scalar(out=ys[t][:, i, :], in0=ys[t][:, i, :], scalar1=quarters[t][:, i : i + 1], scalar2=None, op0=ALU.mult)
+            else:
+                nc.scalar.activation(out=ys[t][:, i, :], in_=ys[t][:, i, :], func=ACT.Copy, scale=quarters[t][:, i : i + 1])
+            nc.sync.dma_start(out=out_0[once[t][1], i * P : (i + 1) * P, :], in_=ys[t][:, i, :])
+
+        def total_weight(n, t):
+            totals[n] = work.tile([P, 1], F32, name="total")
+            nc.vector.tensor_reduce(out=totals[n][:], in_=quarters[t][:, Q:], axis=AX.X, op=ALU.add)
+
+        def bias_share(n):
+            accs[n] = work.tile([P, E], F32, name="acc", bufs=6)
+            nc.scalar.activation(out=accs[n][:], in_=bias_all[twice[n][1]][:], func=ACT.Copy, scale=totals[n][:])
+
+        def add_word(n, t, i):
+            j, h = twice[n]
+            nc.vector.scalar_tensor_tensor(
+                out=accs[n][:], in0=banks["b", n, i][:], scalar=quarters[t][:, Q + i : Q + i + 1], in1=accs[n][:], op0=ALU.mult, op1=ALU.add
+            )
+            if i == Q - 1:
+                nc.sync.dma_start(out=out_1[h, j * P : (j + 1) * P, :], in_=accs[n][:])
+
+        def pool_scale(t, i):
+            j, h = once[t]
+            nc.gpsimd.tensor_scalar(
+                out=ys[t][:, i, :], in0=ys[t][:, i, :], scalar1=quarters[t][:, i : i + 1], scalar2=0.0, op0=ALU.mult, op1=ALU.add
+            )
+            if j is None:
+                nc.sync.dma_start(out=out_0[h, i * P : (i + 1) * P, :], in_=ys[t][:, i, :])
+
+        def pool_add(t, i, k):
+            j, h = once[t]
+            nc.gpsimd.tensor_tensor(out=ys[t][:, i, :], in0=ys[t][:, i, :], in1=ys[t][:, k, :], op=ALU.add)
+            if k == 2:
+                nc.sync.dma_start(out=out_1[h, j * P : (j + 1) * P, :], in_=ys[t][:, 0, :])
+
+        def drain(passes):
+            while backlog and passes > 0:
+                cost, call, args = backlog.pop(0)
+                call(*args)
+                passes -= cost
+
+        for key in units[:2]:
+            for half in range(2):
+                turn(key, half)
+                copy_half(key, half, half == 1)
+            quantise(key)
+        for half in range(2):
+            turn(units[2], half)
+        bias_columns()
+
+        for t in range(n_steps + 1):
+            plain = once[t] if t < n_steps else None
+            f, m, k = t - FIRST, t - FIRST - 1, t - FIRST - LAG
+            front, middle, back = [0 <= n < len(twice) for n in (f, m, k)]
+            fresh = ready[t - 1]
+            cols = slice(0, 2 * Q if middle else Q)
+            if middle:
+                fold_sum(m, t - 1)
+            for kind, i in (("p", 0), ("b", 0), ("f", 0), ("f", 1), ("p", 1), ("f", 2), ("b", 1), ("f", 3), ("p", 2), ("b", 2), ("p", 3), ("b", 3)):
+                if kind == "p" and plain:
+                    mm(("p", t, i), ("F", plain[0]), i, ("W", plain[1]))
+                if kind == "b" and back:
+                    mm(("b", k, i), ("F", twice[k][0]), i, ("W", twice[k][1]))
+                if kind == "f" and front:
+                    mm(("f", f, i), ("W", twice[f][1]), i, ("F", twice[f][0]))
+            for key in fresh:
+                copy_half(key, 0, VC and front and not back and key == fresh[0])
+                copy_half(key, 1, not back)
+            for i in range(Q):
+                if front:
+                    turned_squares(f, i)
+                if i == C_AT and t > 0:
+                    clamp(t - 1, cols)
+                if i == C_AT + 1 and t > 0:
+                    root(t - 1, cols)
+                if plain:
+                    add_bias(t, i)
+                if i == I_AT and t > 0:
+                    invert(t - 1, cols)
+                    drain(20)
+                if back:
+                    add_word(k, t - LAG, i)
+                if i < len(fresh):
+                    quantise(fresh[i])
+                if i == I_AT and middle:
+                    total_weight(m, t - 1)
+            for key in ready[t]:
+                for half in range(2):
+                    turn(key, half)
+            if front:
+                fold(f, range(Q))
+            for i in range(Q):
+                if plain:
+                    row_squares(t, i)
+                if i == SHARE_AT and middle:
+                    bias_share(m)
+                if t - 1 in senses[HEADS - SCALAR_Q :]:
+                    scalar_scale(t - 1, i, t == n_steps and i % 2 == 0)
+        drain(1000)

@@ -19,17 +19,25 @@ AX = mybir.AxisListType
 
 P = 128
 Q = 4
-POOL_PASSES = (0, 8)
-N_POOL = 11
-SCALAR_Q = 1
-V_COPY_STEPS = 4
-FIRST = 2
+KINDS = "ZZZZZZqZqZqZqZqq"
+WHO = ("GGGG", "GGGG", "GGGG", "GGSS", "SSSS", "SVSV")
+LAST_FRONT = 14
 LAG = 2
 SHARE_AT = 1
-VC = 1
 C_AT = 0
 I_AT = 1
-SENSES = (4, 8, 11, 14, 15, 16)
+GLAG = 1
+VSCALE = 0
+MERGE = 99
+DEFER = 1
+LATE_OFF = 1
+VLATE = 1
+LASTORD = 0
+VCOPY = (1, 2, 2)
+PREP = (0, 1, 2, 3)
+INV = 3
+QPOS = 3
+TAIL = 'SGSV'
 
 
 def tile_biencodermodel_pa_kernel(tc, feature, aspect_v, W, b, out_0, out_1):
@@ -40,22 +48,29 @@ def tile_biencodermodel_pa_kernel(tc, feature, aspect_v, W, b, out_0, out_1):
         psum = ctx.enter_context(tc.psum_pool(name="psum", bufs=1))
         ctx.enter_context(tc.manual_schedule())
 
-        units = [("W", 0), ("F", 0), ("F", 1), ("W", 1), ("F", None), ("F", 2), ("W", 2), ("F", 3), ("W", 3), ("W", 4), ("W", 5)]
+        batches = [
+            [("W", 0)], [("F", 0)], [("F", 1)], [("W", 1)],
+            [("F", 2), ("F", 3)], [("W", 2), ("W", 3)], [("W", 4), ("W", 5)], [("F", None)],
+        ]
+        units = [key for batch in batches for key in batch]
         sources = {("W", h): W[h].rearrange("(c p) k -> p c k", p=P) for h in range(HEADS)}
         sources.update({("F", j): feature[j * P : (j + 1) * P] for j in range(Q)})
         sources[("F", None)] = aspect_v.rearrange("(j p) k -> p j k", p=P)
         means = sorted(
             [(j, h) for j in range(Q) for h in range(HEADS)], key=lambda g: max(units.index(("F", g[0])), units.index(("W", g[1])))
         )
-        n_steps = N_POOL + HEADS
-        senses = list(SENSES)
-        once, twice = [], []
-        for t in range(n_steps):
-            once.append((None, senses.index(t)) if t in senses else means.pop(0))
-            if t >= FIRST and len(twice) < Q * HEADS - N_POOL:
-                twice.append(means.pop(0))
-        ready = {-1: units[2:3], 0: units[3:5], 1: units[5:7]}
-        ready.update({t: units[t + 5 : t + 6] for t in range(2, n_steps + 1)})
+        n_steps = len(KINDS)
+        once, crosswise, again = [], {}, {}
+        for t, kind in enumerate(KINDS):
+            once.append(means.pop(0) if kind in "ZX" else (None, len([g for g in once if g[0] is None])))
+            if kind == "X":
+                again[t] = once[t], 0
+            elif 1 <= t <= LAST_FRONT:
+                crosswise[t] = means.pop(0)
+                again[t] = crosswise[t], Q
+        assert not means
+        ready = {t: [batches[4 + PREP.index(t)]] if t in PREP else [] for t in range(n_steps + 1)}
+        ready[-1] = batches[2:4]
 
         bias_rows = keep.tile([P, P], BF16, name="bias_rows")
         nc.vector.memset(bias_rows[:], 0.0)
@@ -63,7 +78,11 @@ def tile_biencodermodel_pa_kernel(tc, feature, aspect_v, W, b, out_0, out_1):
         raw, bias_all = {}, {}
         for key in units:
             raw[key] = keep.tile([P, Q, H], BF16, name="raw_%s%s" % key)
-            nc.sync.dma_start(out=raw[key][:], in_=sources[key])
+            if len(raw) <= 2:
+                for half in (slice(0, 2), slice(2, Q)):
+                    nc.sync.dma_start(out=raw[key][:, half, :], in_=sources[key][:, half, :])
+            else:
+                nc.sync.dma_start(out=raw[key][:], in_=sources[key])
             if key == ("F", 0) or (key[0] == "W" and key[1] > 0):
                 h = key[1]
                 bias_all[h] = keep.tile([P, E], BF16, name="bias_all%d" % h)
@@ -75,24 +94,34 @@ def tile_biencodermodel_pa_kernel(tc, feature, aspect_v, W, b, out_0, out_1):
         make_identity(nc, ident_bf[:])
         bias_col = keep.tile([P, HEADS * Q], F32, name="bias_col")
 
-        codes, scales, grouped, turned = {}, {}, {}, {}
+        codes, scales, grouped, turned = {}, {}, {}, []
 
-        def turn(key, half):
-            if half == 0:
-                grouped[key] = work.tile([P, Q * P * 4], BF16, name="grouped", align_bytes=64, bufs=4)
-            bank = psum.tile([P, 2, 2, P], F32, name="bank", bufs=8)
-            for i in range(2):
-                words = raw[key][:, 2 * half + i, :].bitcast(F32)
-                for u in range(2):
-                    nc.tensor.transpose(bank[:, i, u, :], words[:, u::2], ident[:])
-            dst = grouped[key][:].bitcast(F32).rearrange("p (i r u) -> p i r u", i=Q, u=2)
-            turned[key, half] = dst[:, 2 * half : 2 * half + 2], bank[:].rearrange("p i u r -> p i r u")
+        def turn(batch):
+            grouped[batch[0]] = work.tile([P, len(batch) * Q * P * 4], BF16, name="grouped", align_bytes=64)
+            dst = grouped[batch[0]][:].bitcast(F32).rearrange("p (i r u) -> p i r u", r=P, u=2)
+            for n in range(2 * len(batch)):
+                bank = psum.tile([P, 2, 2, P], F32, name="bank", bufs=8)
+                for i in range(2):
+                    words = raw[batch[n // 2]][:, 2 * (n % 2) + i, :].bitcast(F32)
+                    for u in range(2):
+                        nc.tensor.transpose(bank[:, i, u, :], words[:, u::2], ident[:])
+                turned.append((dst[:, 2 * n : 2 * n + 2], bank[:].rearrange("p i u r -> p i r u")))
 
-        def quantise(key):
-            codes[key] = keep.tile([P, Q * P], U32, name="codes_%s%s" % key, align_bytes=64)
-            scales[key] = keep.tile([P, Q * P], U8, name="scales_%s%s" % key, align_bytes=64)
+        def quantise(batch, part=0, parts=1):
+            width = len(batch) * Q * P
+            if part == 0:
+                words = keep.tile([P, width], U32, name="codes_%s%s" % batch[0], align_bytes=64)
+                plane = keep.tile([P, width], U8, name="scales_%s%s" % batch[0], align_bytes=64)
+                packed[batch[0]] = words, plane
+                for n, key in enumerate(batch):
+                    codes[key] = words[:, n * Q * P : (n + 1) * Q * P]
+                    scales[key] = plane[:, n * Q * P : (n + 1) * Q * P]
+            words, plane = packed[batch[0]]
+            lo, hi = part * width // parts, (part + 1) * width // parts
             nc.vector.quantize_mx(
-                out=codes[key][:].bitcast(E4M3X4 if key[0] == "W" else E5M2X4), scales=scales[key][:], in_=grouped[key][:]
+                out=words[:, lo:hi].bitcast(E4M3X4 if batch[0][0] == "W" else E5M2X4),
+                scales=plane[:, lo:hi],
+                in_=grouped[batch[0]][:, 4 * lo : 4 * hi],
             )
 
         def product(stat, i, mov):
@@ -102,27 +131,29 @@ def tile_biencodermodel_pa_kernel(tc, feature, aspect_v, W, b, out_0, out_1):
                 out=bank[:],
                 lhsT=codes[stat][:, cols].bitcast(E4M3X4 if stat[0] == "W" else E5M2X4),
                 lhsT_scale=scales[stat][:, cols],
-                rhs=codes[mov][:].bitcast(E4M3X4 if mov[0] == "W" else E5M2X4),
-                rhs_scale=scales[mov][:],
+                rhs=codes[mov].bitcast(E4M3X4 if mov[0] == "W" else E5M2X4),
+                rhs_scale=scales[mov],
                 start=True,
                 stop=True,
             )
             return bank
 
         banks, squares, sumsq, ys, quarters, accs, sums, small = {}, {}, {}, {}, {}, {}, {}, {}
-        backlog, totals = [], {}
+        totals, packed, pending = {}, {}, []
 
-        def copy_half(key, half, on_vector):
-            dst, src = turned[key, half]
+        def copy_out(on_vector):
+            dst, src = turned.pop(0)
             if on_vector:
                 nc.vector.tensor_copy(out=dst, in_=src)
             else:
                 nc.scalar.copy(out=dst, in_=src)
 
-        def bias_columns():
-            bank = psum.tile([P, P], BF16, name="bank", bufs=8)
-            nc.tensor.transpose(bank[:], bias_rows[:], ident_bf[:])
-            nc.vector.tensor_copy(out=bias_col[:], in_=bank[:, 0 : HEADS * Q])
+        def bias_columns_turn():
+            banks["bias"] = psum.tile([P, P], BF16, name="bank", bufs=8)
+            nc.tensor.transpose(banks["bias"][:], bias_rows[:], ident_bf[:])
+
+        def bias_columns_copy():
+            nc.vector.tensor_copy(out=bias_col[:], in_=banks["bias"][:, 0 : HEADS * Q])
 
         def mm(name, stat, i, mov):
             banks[name] = product(stat, i, mov)
@@ -144,7 +175,7 @@ def tile_biencodermodel_pa_kernel(tc, feature, aspect_v, W, b, out_0, out_1):
         def turned_squares(n, i):
             if i == 0:
                 squares[n] = work.tile([P, Q, E], F32, name="squares")
-            col = Q * twice[n][1] + i
+            col = Q * crosswise[n][1] + i
             nc.scalar.activation(out=squares[n][:, i, :], in_=banks["f", n, i][:], func=ACT.Square, bias=bias_col[:, col : col + 1])
 
         def fold(n, words):
@@ -171,7 +202,7 @@ def tile_biencodermodel_pa_kernel(tc, feature, aspect_v, W, b, out_0, out_1):
         def root(t, cols):
             norms = work.tile([P, 2 * Q], F32, name="norms")
             parts = [(cols, 16.0)]
-            if t in senses:
+            if once[t][0] is None:
                 parts = [(slice(0, Q), 1.0)] + ([(slice(Q, 2 * Q), 16.0)] if cols.stop > Q else [])
             for part, factor in parts:
                 nc.scalar.activation(out=norms[:, part], in_=small[t][:, part], func=ACT.Sqrt, scale=factor, bias=factor * EPS * EPS)
@@ -181,110 +212,143 @@ def tile_biencodermodel_pa_kernel(tc, feature, aspect_v, W, b, out_0, out_1):
             quarters[t] = work.tile([P, 2 * Q], F32, name="quarter", bufs=8)
             nc.vector.reciprocal(out=quarters[t][:, cols], in_=small[t][:, cols])
             j, h = once[t]
-            if t in senses[HEADS - SCALAR_Q :]:
-                return
-            backlog.extend([(1, pool_scale, (t, i)) for i in range(Q)])
-            if j is not None:
-                backlog.extend([(2, pool_add, (t, i, k)) for i, k in ((0, 1), (2, 3), (0, 2))])
+            if KINDS[t] in "Zq":
+                for i in range(Q):
+                    if t < VSCALE:
+                        nc.vector.tensor_scalar(out=ys[t][:, i, :], in0=ys[t][:, i, :], scalar1=quarters[t][:, i : i + 1], scalar2=None, op0=ALU.mult)
+                    elif KINDS[t] == "Z" or WHO[h][i] == "G":
+                        pool_scale(t, i)
+                    if i == 0:
+                        finish()
+            if KINDS[t] == "Z":
+                if t >= MERGE:
+                    nc.gpsimd.tensor_tensor(out=ys[t][:, 0:2, :], in0=ys[t][:, 0:2, :], in1=ys[t][:, 2:4, :], op=ALU.add)
+                else:
+                    for i in range(2):
+                        nc.gpsimd.tensor_tensor(out=ys[t][:, i, :], in0=ys[t][:, i, :], in1=ys[t][:, i + 2, :], op=ALU.add)
+                pending.append(t)
+                if not DEFER or KINDS[t + 1] == "q" and WHO[once[t + 1][1]][0] != "G":
+                    finish()
+
+        def finish():
+            while pending:
+                t = pending.pop()
+                nc.gpsimd.tensor_tensor(out=ys[t][:, 0, :], in0=ys[t][:, 0, :], in1=ys[t][:, 1, :], op=ALU.add)
+
+        def pool_store(t):
+            j, h = once[t]
+            if j is None:
+                for i in [i for i in range(Q) if WHO[h][i] == "G"]:
+                    nc.sync.dma_start(out=out_0[h, i * P : (i + 1) * P, :], in_=ys[t][:, i, :])
+            else:
+                nc.sync.dma_start(out=out_1[h, j * P : (j + 1) * P, :], in_=ys[t][:, 0, :])
 
         def scalar_scale(t, i, on_vector):
-            if on_vector:
+            if on_vector == "G":
+                pool_scale(t, i)
+            elif on_vector == "V":
                 nc.vector.tensor_scalar(out=ys[t][:, i, :], in0=ys[t][:, i, :], scalar1=quarters[t][:, i : i + 1], scalar2=None, op0=ALU.mult)
             else:
                 nc.scalar.activation(out=ys[t][:, i, :], in_=ys[t][:, i, :], func=ACT.Copy, scale=quarters[t][:, i : i + 1])
             nc.sync.dma_start(out=out_0[once[t][1], i * P : (i + 1) * P, :], in_=ys[t][:, i, :])
 
-        def total_weight(n, t):
-            totals[n] = work.tile([P, 1], F32, name="total")
-            nc.vector.tensor_reduce(out=totals[n][:], in_=quarters[t][:, Q:], axis=AX.X, op=ALU.add)
+        def total_weight(t):
+            first = again[t][1]
+            totals[t] = work.tile([P, 1], F32, name="total")
+            nc.vector.tensor_reduce(out=totals[t][:], in_=quarters[t][:, first : first + Q], axis=AX.X, op=ALU.add)
 
-        def bias_share(n):
-            accs[n] = work.tile([P, E], F32, name="acc", bufs=6)
-            nc.scalar.activation(out=accs[n][:], in_=bias_all[twice[n][1]][:], func=ACT.Copy, scale=totals[n][:])
+        def bias_share(t):
+            accs[t] = work.tile([P, E], F32, name="acc", bufs=6)
+            nc.scalar.activation(out=accs[t][:], in_=bias_all[again[t][0][1]][:], func=ACT.Copy, scale=totals[t][:])
 
-        def add_word(n, t, i):
-            j, h = twice[n]
+        def add_word(t, i):
+            (j, h), first = again[t]
             nc.vector.scalar_tensor_tensor(
-                out=accs[n][:], in0=banks["b", n, i][:], scalar=quarters[t][:, Q + i : Q + i + 1], in1=accs[n][:], op0=ALU.mult, op1=ALU.add
+                out=accs[t][:], in0=banks["b", t, i][:], scalar=quarters[t][:, first + i : first + i + 1], in1=accs[t][:], op0=ALU.mult, op1=ALU.add
             )
             if i == Q - 1:
-                nc.sync.dma_start(out=out_1[h, j * P : (j + 1) * P, :], in_=accs[n][:])
+                nc.sync.dma_start(out=out_1[h, j * P : (j + 1) * P, :], in_=accs[t][:])
 
         def pool_scale(t, i):
             j, h = once[t]
             nc.gpsimd.tensor_scalar(
                 out=ys[t][:, i, :], in0=ys[t][:, i, :], scalar1=quarters[t][:, i : i + 1], scalar2=0.0, op0=ALU.mult, op1=ALU.add
             )
-            if j is None:
-                nc.sync.dma_start(out=out_0[h, i * P : (i + 1) * P, :], in_=ys[t][:, i, :])
 
-        def pool_add(t, i, k):
-            j, h = once[t]
-            nc.gpsimd.tensor_tensor(out=ys[t][:, i, :], in0=ys[t][:, i, :], in1=ys[t][:, k, :], op=ALU.add)
-            if k == 2:
-                nc.sync.dma_start(out=out_1[h, j * P : (j + 1) * P, :], in_=ys[t][:, 0, :])
-
-        def drain(passes):
-            while backlog and passes > 0:
-                cost, call, args = backlog.pop(0)
-                call(*args)
-                passes -= cost
-
-        for key in units[:2]:
-            for half in range(2):
-                turn(key, half)
-                copy_half(key, half, half == 1)
-            quantise(key)
+        turn(batches[0])
+        copy_out(False)
+        copy_out(True)
+        quantise(batches[0])
+        turn(batches[1])
         for half in range(2):
-            turn(units[2], half)
-        bias_columns()
+            copy_out(half == 1)
+            quantise(batches[1], half, 2)
+        turn(batches[2])
 
         for t in range(n_steps + 1):
             plain = once[t] if t < n_steps else None
-            f, m, k = t - FIRST, t - FIRST - 1, t - FIRST - LAG
-            front, middle, back = [0 <= n < len(twice) for n in (f, m, k)]
+            front, middle, back = t in crosswise, t - 1 in crosswise, t - LAG in again
+            last = t == n_steps - 1 and LASTORD
             fresh = ready[t - 1]
             cols = slice(0, 2 * Q if middle else Q)
             if middle:
-                fold_sum(m, t - 1)
-            for kind, i in (("p", 0), ("b", 0), ("f", 0), ("f", 1), ("p", 1), ("f", 2), ("b", 1), ("f", 3), ("p", 2), ("b", 2), ("p", 3), ("b", 3)):
+                fold_sum(t - 1, t - 1)
+            order = (("p", 0), ("b", 0), ("f", 0), ("f", 1), ("p", 1), ("f", 2), ("b", 1), ("f", 3), ("p", 2), ("b", 2), ("p", 3), ("b", 3))
+            if last:
+                order = (("p", 0), ("p", 1), ("b", 0), ("p", 2), ("b", 1), ("p", 3), ("b", 2), ("b", 3))
+            for kind, i in order:
                 if kind == "p" and plain:
                     mm(("p", t, i), ("F", plain[0]), i, ("W", plain[1]))
                 if kind == "b" and back:
-                    mm(("b", k, i), ("F", twice[k][0]), i, ("W", twice[k][1]))
+                    mm(("b", t - LAG, i), ("F", again[t - LAG][0][0]), i, ("W", again[t - LAG][0][1]))
                 if kind == "f" and front:
-                    mm(("f", f, i), ("W", twice[f][1]), i, ("F", twice[f][0]))
-            for key in fresh:
-                copy_half(key, 0, VC and front and not back and key == fresh[0])
-                copy_half(key, 1, not back)
-            for i in range(Q):
-                if front:
-                    turned_squares(f, i)
-                if i == C_AT and t > 0:
-                    clamp(t - 1, cols)
-                if i == C_AT + 1 and t > 0:
-                    root(t - 1, cols)
-                if plain:
-                    add_bias(t, i)
-                if i == I_AT and t > 0:
-                    invert(t - 1, cols)
-                    drain(20)
-                if back:
-                    add_word(k, t - LAG, i)
-                if i < len(fresh):
-                    quantise(fresh[i])
-                if i == I_AT and middle:
-                    total_weight(m, t - 1)
-            for key in ready[t]:
-                for half in range(2):
-                    turn(key, half)
+                    mm(("f", t, i), ("W", crosswise[t][1]), i, ("F", crosswise[t][0]))
+            if t == 0:
+                turn(batches[3])
+                bias_columns_turn()
+            on_vector = min(len(turned), VCOPY[t] if t < len(VCOPY) else VLATE)
+            first_half = [(copy_out, (False,)) for n in range(len(turned) - on_vector)]
+            first_half += [(turned_squares, (t, i)) for i in range(Q) if front]
+            if 0 < t < n_steps:
+                first_half.insert(1, (clamp, (t - 1, cols)))
+                first_half.insert(3, (root, (t - 1, cols)))
+            for call, args in first_half:
+                call(*args)
+            vec = [(copy_out, (True,)) for n in range(on_vector)]
+            rows = [(add_bias if kind == "p" else add_word, (t if kind == "p" else t - LAG, i)) for kind, i in order if kind == "p" and plain or kind == "b" and back]
+            if t == 0:
+                vec = rows[:2] + [(quantise, (fresh[0],))] + rows[2:3] + vec + rows[3:] + [(quantise, (fresh[1],)), (bias_columns_copy, ())]
+            else:
+                vec = vec[:1] + rows[:1] + vec[1:] + rows[1:]
+                vec.insert((INV - middle) if plain else 1, (invert, (t - 1, cols)))
+                if t - 1 in again:
+                    vec.insert(INV + 2 - middle, (total_weight, (t - 1,)))
+                if fresh:
+                    vec.insert(len(vec) - QPOS, (quantise, (fresh[0],)))
+            late = [i for i in range(Q) if t > 0 and KINDS[t - 1] == "q" and WHO[once[t - 1][1]][i] == "S"]
+            if not plain:
+                for n, i in enumerate([i for i in range(Q) if WHO[-1][i] == "V"]):
+                    vec.insert(3 + 2 * n, (scalar_scale, (t - 1, i, "V")))
+                for n, i in enumerate(late):
+                    vec.insert(2, (scalar_scale, (t - 1, i, "S")))
+            for call, args in vec:
+                call(*args)
+            for batch in ready[t]:
+                turn(batch)
             if front:
-                fold(f, range(Q))
-            for i in range(Q):
-                if plain:
-                    row_squares(t, i)
-                if i == SHARE_AT and middle:
-                    bias_share(m)
-                if t - 1 in senses[HEADS - SCALAR_Q :]:
-                    scalar_scale(t - 1, i, t == n_steps and i % 2 == 0)
-        drain(1000)
+                fold(t, range(Q))
+            second_half = [(row_squares, (t, i)) for i in range(Q) if plain]
+            if t - 1 in again:
+                second_half.insert(SHARE_AT + 1, (bias_share, (t - 1,)))
+            if t == n_steps - 1:
+                second_half += [(clamp, (t, slice(0, Q))), (root, (t, slice(0, Q)))]
+            if plain:
+                for n, i in enumerate(late[::-1]):
+                    second_half.insert(len(second_half) - 2 * n - LATE_OFF, (scalar_scale, (t - 1, i, "S")))
+            for call, args in second_half:
+                call(*args)
+            if t - 1 - GLAG >= 0 and KINDS[t - 1 - GLAG] in "Zq":
+                pool_store(t - 1 - GLAG)
+        for t in range(n_steps - GLAG, n_steps):
+            if KINDS[t] in "Zq":
+                pool_store(t)

@@ -20,7 +20,7 @@ AX = mybir.AxisListType
 P = 128
 Q = 4
 KINDS = "ZZZZZZqZqZqZqZqq"
-WHO = ("GGGG", "GGGG", "GGGG", "GGSS", "SSSS", "SVSV")
+WHO = ("GGGG", "GGGG", "GGGG", "GGGS", "SSSS", "SVSV")
 LAST_FRONT = 14
 LAG = 2
 SHARE_AT = 1
@@ -28,15 +28,16 @@ C_AT = 0
 I_AT = 1
 GLAG = 1
 VSCALE = 0
-MERGE = 99
+MERGE = 6
 DEFER = 1
+SPREAD_AT = 1
 LATE_OFF = 1
 VLATE = 1
 LASTORD = 0
 VCOPY = (1, 2, 2)
-PREP = (0, 1, 2, 3)
+PREP = (0, 2, 4, 3)
 INV = 3
-QPOS = 3
+QPOS = 2
 TAIL = 'SGSV'
 
 
@@ -72,9 +73,9 @@ def tile_biencodermodel_pa_kernel(tc, feature, aspect_v, W, b, out_0, out_1):
         ready = {t: [batches[4 + PREP.index(t)]] if t in PREP else [] for t in range(n_steps + 1)}
         ready[-1] = batches[2:4]
 
-        bias_rows = keep.tile([P, P], BF16, name="bias_rows")
+        bias_rows = keep.tile([P, E], BF16, name="bias_rows")
         nc.vector.memset(bias_rows[:], 0.0)
-        nc.scalar.dma_start(out=bias_rows[0 : HEADS * Q, :], in_=b.rearrange("h (c p) -> (h c) p", p=P))
+        nc.scalar.dma_start(out=bias_rows[0:HEADS, :], in_=b)
         raw, bias_all = {}, {}
         for key in units:
             raw[key] = keep.tile([P, Q, H], BF16, name="raw_%s%s" % key)
@@ -83,16 +84,12 @@ def tile_biencodermodel_pa_kernel(tc, feature, aspect_v, W, b, out_0, out_1):
                     nc.sync.dma_start(out=raw[key][:, half, :], in_=sources[key][:, half, :])
             else:
                 nc.sync.dma_start(out=raw[key][:], in_=sources[key])
-            if key == ("F", 0) or (key[0] == "W" and key[1] > 0):
-                h = key[1]
-                bias_all[h] = keep.tile([P, E], BF16, name="bias_all%d" % h)
-                nc.sync.dma_start(out=bias_all[h][:], in_=b[h].partition_broadcast(P))
 
         ident = keep.tile([P, P], F32, name="ident")
         make_identity(nc, ident[:])
         ident_bf = keep.tile([P, P], BF16, name="ident_bf")
         make_identity(nc, ident_bf[:])
-        bias_col = keep.tile([P, HEADS * Q], F32, name="bias_col")
+        bias_col = keep.tile([P, Q, HEADS], F32, name="bias_col")
 
         codes, scales, grouped, turned = {}, {}, {}, []
 
@@ -139,7 +136,7 @@ def tile_biencodermodel_pa_kernel(tc, feature, aspect_v, W, b, out_0, out_1):
             return bank
 
         banks, squares, sumsq, ys, quarters, accs, sums, small = {}, {}, {}, {}, {}, {}, {}, {}
-        totals, packed, pending = {}, {}, []
+        totals, packed, pending, spread = {}, {}, [], []
 
         def copy_out(on_vector):
             dst, src = turned.pop(0)
@@ -149,11 +146,27 @@ def tile_biencodermodel_pa_kernel(tc, feature, aspect_v, W, b, out_0, out_1):
                 nc.scalar.copy(out=dst, in_=src)
 
         def bias_columns_turn():
-            banks["bias"] = psum.tile([P, P], BF16, name="bank", bufs=8)
-            nc.tensor.transpose(banks["bias"][:], bias_rows[:], ident_bf[:])
+            banks["bias"] = psum.tile([P, Q, P], BF16, name="bank", bufs=8)
+            for c in range(Q):
+                nc.tensor.transpose(banks["bias"][:, c, :], bias_rows[:, c * P : (c + 1) * P], ident_bf[:])
 
         def bias_columns_copy():
-            nc.vector.tensor_copy(out=bias_col[:], in_=banks["bias"][:, 0 : HEADS * Q])
+            nc.vector.tensor_copy(out=bias_col[:], in_=banks["bias"][:, :, 0:HEADS])
+
+        def spread_bias(pair):
+            bank = psum.tile([P, 2, E], BF16, name="bank", bufs=8)
+            both = keep.tile([P, 2, E], BF16, name="bias_pair%d" % pair)
+            for n in range(2):
+                h = 2 * pair + n
+                nc.tensor.matmul(
+                    out=bank[:, n, :], lhsT=ident_bf[:, h : h + 1].to_broadcast([P, P]), rhs=bias_rows[:], start=True, stop=True
+                )
+                bias_all[h] = both[:, n, :]
+            spread.append((both, bank))
+
+        def spread_copy():
+            both, bank = spread.pop(0)
+            nc.vector.tensor_copy(out=both[:], in_=bank[:])
 
         def mm(name, stat, i, mov):
             banks[name] = product(stat, i, mov)
@@ -166,7 +179,7 @@ def tile_biencodermodel_pa_kernel(tc, feature, aspect_v, W, b, out_0, out_1):
         def add_bias(t, i):
             if i == 0:
                 ys[t] = work.tile([P, Q, E], F32, name="y", bufs=6)
-            nc.vector.tensor_tensor(out=ys[t][:, i, :], in0=banks["p", t, i][:], in1=bias_all[once[t][1]][:], op=ALU.add)
+            nc.vector.tensor_tensor(out=ys[t][:, i, :], in0=banks["p", t, i][:], in1=bias_all[once[t][1]], op=ALU.add)
 
         def row_squares(t, i):
             unread = work.tile([P, E], BF16, name="unread")
@@ -175,8 +188,8 @@ def tile_biencodermodel_pa_kernel(tc, feature, aspect_v, W, b, out_0, out_1):
         def turned_squares(n, i):
             if i == 0:
                 squares[n] = work.tile([P, Q, E], F32, name="squares")
-            col = Q * crosswise[n][1] + i
-            nc.scalar.activation(out=squares[n][:, i, :], in_=banks["f", n, i][:], func=ACT.Square, bias=bias_col[:, col : col + 1])
+            h = crosswise[n][1]
+            nc.scalar.activation(out=squares[n][:, i, :], in_=banks["f", n, i][:], func=ACT.Square, bias=bias_col[:, i, h : h + 1])
 
         def fold(n, words):
             if words[0] == 0:
@@ -200,17 +213,23 @@ def tile_biencodermodel_pa_kernel(tc, feature, aspect_v, W, b, out_0, out_1):
             nc.scalar.activation(out=small[t][:, cols], in_=sumsq[t][:, cols], func=ACT.Relu, bias=-EPS * EPS)
 
         def root(t, cols):
-            norms = work.tile([P, 2 * Q], F32, name="norms")
-            parts = [(cols, 16.0)]
-            if once[t][0] is None:
-                parts = [(slice(0, Q), 1.0)] + ([(slice(Q, 2 * Q), 16.0)] if cols.stop > Q else [])
-            for part, factor in parts:
-                nc.scalar.activation(out=norms[:, part], in_=small[t][:, part], func=ACT.Sqrt, scale=factor, bias=factor * EPS * EPS)
-            small[t] = norms
+            quarters[t] = work.tile([P, 2 * Q], F32, name="quarter", bufs=8)
+            factor = 1.0 if KINDS[t] == "q" else 16.0
+            nc.scalar.activation(
+                out=quarters[t][:, 0:Q], in_=small[t][:, 0:Q], func=ACT.Abs_reciprocal_sqrt, scale=factor, bias=factor * EPS * EPS
+            )
+            if cols.stop > Q:
+                totals[t] = work.tile([P, 1], F32, name="total")
+                nc.scalar.activation(
+                    out=quarters[t][:, Q:],
+                    in_=small[t][:, Q:],
+                    func=ACT.Abs_reciprocal_sqrt,
+                    scale=16.0,
+                    bias=16.0 * EPS * EPS,
+                    accum_out=totals[t][:],
+                )
 
         def invert(t, cols):
-            quarters[t] = work.tile([P, 2 * Q], F32, name="quarter", bufs=8)
-            nc.vector.reciprocal(out=quarters[t][:, cols], in_=small[t][:, cols])
             j, h = once[t]
             if KINDS[t] in "Zq":
                 for i in range(Q):
@@ -259,7 +278,7 @@ def tile_biencodermodel_pa_kernel(tc, feature, aspect_v, W, b, out_0, out_1):
 
         def bias_share(t):
             accs[t] = work.tile([P, E], F32, name="acc", bufs=6)
-            nc.scalar.activation(out=accs[t][:], in_=bias_all[again[t][0][1]][:], func=ACT.Copy, scale=totals[t][:])
+            nc.scalar.activation(out=accs[t][:], in_=bias_all[again[t][0][1]], func=ACT.Copy, scale=totals[t][:])
 
         def add_word(t, i):
             (j, h), first = again[t]
@@ -283,6 +302,8 @@ def tile_biencodermodel_pa_kernel(tc, feature, aspect_v, W, b, out_0, out_1):
         for half in range(2):
             copy_out(half == 1)
             quantise(batches[1], half, 2)
+        spread_bias(0)
+        spread_copy()
         turn(batches[2])
 
         for t in range(n_steps + 1):
@@ -321,10 +342,10 @@ def tile_biencodermodel_pa_kernel(tc, feature, aspect_v, W, b, out_0, out_1):
             else:
                 vec = vec[:1] + rows[:1] + vec[1:] + rows[1:]
                 vec.insert((INV - middle) if plain else 1, (invert, (t - 1, cols)))
-                if t - 1 in again:
-                    vec.insert(INV + 2 - middle, (total_weight, (t - 1,)))
                 if fresh:
                     vec.insert(len(vec) - QPOS, (quantise, (fresh[0],)))
+            if t == SPREAD_AT + 1:
+                vec = [(spread_copy, ())] + vec[:2] + [(spread_copy, ())] + vec[2:]
             late = [i for i in range(Q) if t > 0 and KINDS[t - 1] == "q" and WHO[once[t - 1][1]][i] == "S"]
             if not plain:
                 for n, i in enumerate([i for i in range(Q) if WHO[-1][i] == "V"]):
@@ -335,6 +356,9 @@ def tile_biencodermodel_pa_kernel(tc, feature, aspect_v, W, b, out_0, out_1):
                 call(*args)
             for batch in ready[t]:
                 turn(batch)
+            if t == SPREAD_AT:
+                spread_bias(1)
+                spread_bias(2)
             if front:
                 fold(t, range(Q))
             second_half = [(row_squares, (t, i)) for i in range(Q) if plain]

@@ -11,34 +11,22 @@ F32 = mybir.dt.float32
 BF16 = mybir.dt.bfloat16
 U32 = mybir.dt.uint32
 U8 = mybir.dt.uint8
-E4M3X4 = mybir.dt.float8_e4m3fn_x4
-E5M2X4 = mybir.dt.float8_e5m2_x4
+FORMAT = {"W": mybir.dt.float8_e4m3fn_x4, "X": mybir.dt.float8_e5m2_x4}
 ALU = mybir.AluOpType
 ACT = mybir.ActivationFunctionType
 AX = mybir.AxisListType
 
 P = 128
 Q = 4
-KINDS = "ZZZZZZqZqZqZqZqq"
-WHO = ("GGGG", "GGGG", "GGGG", "GGGS", "SSSS", "SVSV")
-LAST_FRONT = 14
+BANKS = 8
+
+DIRECT_MEANS = 10
+STEPS = DIRECT_MEANS + HEADS
+FIRST_SENSE_STEP = 6
+SENSE_STEPS = list(range(FIRST_SENSE_STEP, STEPS, 2)) + [STEPS - 1]
 LAG = 2
-SHARE_AT = 1
-C_AT = 0
-I_AT = 1
-GLAG = 1
-VSCALE = 0
-MERGE = 6
-DEFER = 1
-SPREAD_AT = 1
-LATE_OFF = 1
-VLATE = 1
-LASTORD = 0
-VCOPY = (1, 2, 2)
-PREP = (0, 2, 4, 3)
-INV = 3
-QPOS = 2
-TAIL = 'SGSV'
+POOL_SENSE_TILES = 15
+VECTOR_START_STEPS = range(8, STEPS - LAG, 2)
 
 
 def tile_biencodermodel_pa_kernel(tc, feature, aspect_v, W, b, out_0, out_1):
@@ -46,44 +34,41 @@ def tile_biencodermodel_pa_kernel(tc, feature, aspect_v, W, b, out_0, out_1):
     with ExitStack() as ctx:
         keep = ctx.enter_context(tc.tile_pool(name="keep", bufs=1))
         work = ctx.enter_context(tc.tile_pool(name="work", bufs=2))
-        psum = ctx.enter_context(tc.psum_pool(name="psum", bufs=1))
+        psum = ctx.enter_context(tc.psum_pool(name="psum", bufs=BANKS))
         ctx.enter_context(tc.manual_schedule())
 
-        batches = [
-            [("W", 0)], [("F", 0)], [("F", 1)], [("W", 1)],
-            [("F", 2), ("F", 3)], [("W", 2), ("W", 3)], [("W", 4), ("W", 5)], [("F", None)],
-        ]
-        units = [key for batch in batches for key in batch]
+        units = [("W", 0), ("X", 0), ("X", 1), ("W", 1), ("X", 2), ("X", 3), ("W", 2), ("X", None)]
+        units += [("W", h) for h in range(3, HEADS)]
         sources = {("W", h): W[h].rearrange("(c p) k -> p c k", p=P) for h in range(HEADS)}
-        sources.update({("F", j): feature[j * P : (j + 1) * P] for j in range(Q)})
-        sources[("F", None)] = aspect_v.rearrange("(j p) k -> p j k", p=P)
+        sources.update({("X", j): feature[j * P : (j + 1) * P] for j in range(Q)})
+        sources["X", None] = aspect_v.rearrange("(j p) k -> p j k", p=P)
+
         means = sorted(
-            [(j, h) for j in range(Q) for h in range(HEADS)], key=lambda g: max(units.index(("F", g[0])), units.index(("W", g[1])))
+            [(j, h) for j in range(Q) for h in range(HEADS)],
+            key=lambda job: max(units.index(("X", job[0])), units.index(("W", job[1]))),
         )
-        n_steps = len(KINDS)
-        once, crosswise, again = [], {}, {}
-        for t, kind in enumerate(KINDS):
-            once.append(means.pop(0) if kind in "ZX" else (None, len([g for g in once if g[0] is None])))
-            if kind == "X":
-                again[t] = once[t], 0
-            elif 1 <= t <= LAST_FRONT:
+        direct, crosswise = [], {}
+        for t in range(STEPS):
+            direct.append((None, SENSE_STEPS.index(t)) if t in SENSE_STEPS else means.pop(0))
+            if 1 <= t <= STEPS - LAG:
                 crosswise[t] = means.pop(0)
-                again[t] = crosswise[t], Q
         assert not means
-        ready = {t: [batches[4 + PREP.index(t)]] if t in PREP else [] for t in range(n_steps + 1)}
-        ready[-1] = batches[2:4]
+        turned_in = {t: units[t + 4] for t in range(len(units) - 4)}
+
+        def scaler(h, i):
+            if Q * h + i < POOL_SENSE_TILES:
+                return "gpsimd"
+            return "vector" if h == HEADS - 1 and i % 2 == 1 else "scalar"
 
         bias_rows = keep.tile([P, E], BF16, name="bias_rows")
         nc.vector.memset(bias_rows[:], 0.0)
         nc.scalar.dma_start(out=bias_rows[0:HEADS, :], in_=b)
-        raw, bias_all = {}, {}
-        for key in units:
-            raw[key] = keep.tile([P, Q, H], BF16, name="raw_%s%s" % key)
-            if len(raw) <= 2:
-                for half in (slice(0, 2), slice(2, Q)):
-                    nc.sync.dma_start(out=raw[key][:, half, :], in_=sources[key][:, half, :])
-            else:
-                nc.sync.dma_start(out=raw[key][:], in_=sources[key])
+
+        raw = {}
+        for unit in units:
+            raw[unit] = keep.tile([P, Q, H], BF16, name="raw_%s%s" % unit)
+            for part in (slice(0, 2), slice(2, Q)) if unit in units[:2] else (slice(0, Q),):
+                nc.sync.dma_start(out=raw[unit][:, part, :], in_=sources[unit][:, part, :])
 
         ident = keep.tile([P, P], F32, name="ident")
         make_identity(nc, ident[:])
@@ -91,288 +76,296 @@ def tile_biencodermodel_pa_kernel(tc, feature, aspect_v, W, b, out_0, out_1):
         make_identity(nc, ident_bf[:])
         bias_col = keep.tile([P, Q, HEADS], F32, name="bias_col")
 
-        codes, scales, grouped, turned = {}, {}, {}, []
+        grouped, codes, scales, bias_wide = {}, {}, {}, {}
+        banks, squares, folded, biased, sums = {}, {}, {}, {}, {}
+        sumsq, excess, weights, totals = {}, {}, {}, {}
+        to_copy, to_spread, last_add = [], [], []
 
-        def turn(batch):
-            grouped[batch[0]] = work.tile([P, len(batch) * Q * P * 4], BF16, name="grouped", align_bytes=64)
-            dst = grouped[batch[0]][:].bitcast(F32).rearrange("p (i r u) -> p i r u", r=P, u=2)
-            for n in range(2 * len(batch)):
-                bank = psum.tile([P, 2, 2, P], F32, name="bank", bufs=8)
+
+        def turn(unit, halves=(0, 1)):
+            if halves[0] == 0:
+                grouped[unit] = work.tile([P, Q * P * 4], BF16, name="grouped", align_bytes=64, bufs=3)
+            pairs = grouped[unit][:].bitcast(F32).rearrange("p (i r u) -> p i r u", r=P, u=2)
+            for half in halves:
+                bank = psum.tile([P, 2, 2, P], F32, name="bank")
                 for i in range(2):
-                    words = raw[batch[n // 2]][:, 2 * (n % 2) + i, :].bitcast(F32)
+                    words = raw[unit][:, 2 * half + i, :].bitcast(F32)
                     for u in range(2):
                         nc.tensor.transpose(bank[:, i, u, :], words[:, u::2], ident[:])
-                turned.append((dst[:, 2 * n : 2 * n + 2], bank[:].rearrange("p i u r -> p i r u")))
+                to_copy.append((pairs[:, 2 * half : 2 * half + 2], bank[:].rearrange("p i u r -> p i r u")))
 
-        def quantise(batch, part=0, parts=1):
-            width = len(batch) * Q * P
-            if part == 0:
-                words = keep.tile([P, width], U32, name="codes_%s%s" % batch[0], align_bytes=64)
-                plane = keep.tile([P, width], U8, name="scales_%s%s" % batch[0], align_bytes=64)
-                packed[batch[0]] = words, plane
-                for n, key in enumerate(batch):
-                    codes[key] = words[:, n * Q * P : (n + 1) * Q * P]
-                    scales[key] = plane[:, n * Q * P : (n + 1) * Q * P]
-            words, plane = packed[batch[0]]
-            lo, hi = part * width // parts, (part + 1) * width // parts
-            nc.vector.quantize_mx(
-                out=words[:, lo:hi].bitcast(E4M3X4 if batch[0][0] == "W" else E5M2X4),
-                scales=plane[:, lo:hi],
-                in_=grouped[batch[0]][:, 4 * lo : 4 * hi],
-            )
-
-        def product(stat, i, mov):
-            bank = psum.tile([P, E], F32, name="bank", bufs=8)
-            cols = slice(i * P, (i + 1) * P)
-            nc.tensor.matmul_mx(
-                out=bank[:],
-                lhsT=codes[stat][:, cols].bitcast(E4M3X4 if stat[0] == "W" else E5M2X4),
-                lhsT_scale=scales[stat][:, cols],
-                rhs=codes[mov].bitcast(E4M3X4 if mov[0] == "W" else E5M2X4),
-                rhs_scale=scales[mov],
-                start=True,
-                stop=True,
-            )
-            return bank
-
-        banks, squares, sumsq, ys, quarters, accs, sums, small = {}, {}, {}, {}, {}, {}, {}, {}
-        totals, packed, pending, spread = {}, {}, [], []
-
-        def copy_out(on_vector):
-            dst, src = turned.pop(0)
-            if on_vector:
+        def copy_out(engine):
+            dst, src = to_copy.pop(0)
+            if engine == "vector":
                 nc.vector.tensor_copy(out=dst, in_=src)
             else:
                 nc.scalar.copy(out=dst, in_=src)
 
-        def bias_columns_turn():
-            banks["bias"] = psum.tile([P, Q, P], BF16, name="bank", bufs=8)
-            for c in range(Q):
-                nc.tensor.transpose(banks["bias"][:, c, :], bias_rows[:, c * P : (c + 1) * P], ident_bf[:])
+        def quantise(unit, rows=slice(0, Q * P)):
+            if rows.start == 0:
+                codes[unit] = keep.tile([P, Q * P], U32, name="codes_%s%s" % unit, align_bytes=64)
+                scales[unit] = keep.tile([P, Q * P], U8, name="scales_%s%s" % unit, align_bytes=64)
+            nc.vector.quantize_mx(
+                out=codes[unit][:, rows].bitcast(FORMAT[unit[0]]),
+                scales=scales[unit][:, rows],
+                in_=grouped[unit][:, 4 * rows.start : 4 * rows.stop],
+            )
 
-        def bias_columns_copy():
-            nc.vector.tensor_copy(out=bias_col[:], in_=banks["bias"][:, :, 0:HEADS])
+
+        def bias_on_all_partitions(out, h):
+            nc.tensor.matmul(
+                out=out, lhsT=ident_bf[:, h : h + 1].to_broadcast([P, P]), rhs=bias_rows[:], start=True, stop=True
+            )
 
         def spread_bias(pair):
-            bank = psum.tile([P, 2, E], BF16, name="bank", bufs=8)
+            bank = psum.tile([P, 2, E], BF16, name="bank")
             both = keep.tile([P, 2, E], BF16, name="bias_pair%d" % pair)
             for n in range(2):
-                h = 2 * pair + n
-                nc.tensor.matmul(
-                    out=bank[:, n, :], lhsT=ident_bf[:, h : h + 1].to_broadcast([P, P]), rhs=bias_rows[:], start=True, stop=True
-                )
-                bias_all[h] = both[:, n, :]
-            spread.append((both, bank))
+                bias_on_all_partitions(bank[:, n, :], 2 * pair + n)
+                bias_wide[2 * pair + n] = both[:, n, :]
+            to_spread.append((both, bank))
 
         def spread_copy():
-            both, bank = spread.pop(0)
+            both, bank = to_spread.pop(0)
             nc.vector.tensor_copy(out=both[:], in_=bank[:])
 
-        def mm(name, stat, i, mov):
-            banks[name] = product(stat, i, mov)
 
-        def stats(t):
-            if t not in sumsq:
-                sumsq[t] = work.tile([P, 2 * Q], F32, name="sumsq", bufs=3)
-            return sumsq[t]
+        def products(t, order):
+            for kind, i in order:
+                j, h = {"d": direct[t : t + 1], "f": [crosswise.get(t)], "s": [crosswise.get(t - LAG)]}[kind][0]
+                stationary, moving = (("W", h), ("X", j)) if kind == "f" else (("X", j), ("W", h))
+                cols = slice(i * P, (i + 1) * P)
+                banks[kind, t, i] = psum.tile([P, E], F32, name="bank")
+                nc.tensor.matmul_mx(
+                    out=banks[kind, t, i][:],
+                    lhsT=codes[stationary][:, cols].bitcast(FORMAT[stationary[0]]),
+                    lhsT_scale=scales[stationary][:, cols],
+                    rhs=codes[moving][:].bitcast(FORMAT[moving[0]]),
+                    rhs_scale=scales[moving][:],
+                    start=True,
+                    stop=True,
+                )
+
 
         def add_bias(t, i):
             if i == 0:
-                ys[t] = work.tile([P, Q, E], F32, name="y", bufs=6)
-            nc.vector.tensor_tensor(out=ys[t][:, i, :], in0=banks["p", t, i][:], in1=bias_all[once[t][1]], op=ALU.add)
+                biased[t] = work.tile([P, Q, E], F32, name="biased", bufs=6)
+            nc.vector.tensor_tensor(out=biased[t][:, i, :], in0=banks["d", t, i][:], in1=bias_wide[direct[t][1]], op=ALU.add)
 
         def row_squares(t, i):
-            unread = work.tile([P, E], BF16, name="unread")
-            nc.scalar.activation(out=unread[:], in_=ys[t][:, i, :], func=ACT.Square, accum_out=stats(t)[:, i : i + 1])
-
-        def turned_squares(n, i):
             if i == 0:
-                squares[n] = work.tile([P, Q, E], F32, name="squares")
-            h = crosswise[n][1]
-            nc.scalar.activation(out=squares[n][:, i, :], in_=banks["f", n, i][:], func=ACT.Square, bias=bias_col[:, i, h : h + 1])
+                sumsq[t] = work.tile([P, 2 * Q], F32, name="sumsq", bufs=3)
+            unread = work.tile([P, E], BF16, name="unread")
+            nc.scalar.activation(out=unread[:], in_=biased[t][:, i, :], func=ACT.Square, accum_out=sumsq[t][:, i : i + 1])
 
-        def fold(n, words):
-            if words[0] == 0:
-                sums[n] = psum.tile([P, Q, P], F32, name="bank", bufs=8)
-            for l in words:
+        def column_squares(t, c):
+            if c == 0:
+                squares[t] = work.tile([P, Q, E], F32, name="squares")
+            h = crosswise[t][1]
+            nc.scalar.activation(out=squares[t][:, c, :], in_=banks["f", t, c][:], func=ACT.Square, bias=bias_col[:, c, h : h + 1])
+
+        def fold(t):
+            folded[t] = psum.tile([P, Q, P], F32, name="bank")
+            for l in range(L):
                 for c in range(Q):
                     nc.tensor.matmul(
-                        out=sums[n][:, l, :],
-                        lhsT=squares[n][:, c, l * P : (l + 1) * P],
+                        out=folded[t][:, l, :],
+                        lhsT=squares[t][:, c, l * P : (l + 1) * P],
                         rhs=ident[:],
                         start=(c == 0),
                         stop=(c == Q - 1),
                         is_transpose=True,
                     )
 
-        def fold_sum(n, t):
-            nc.vector.tensor_reduce(out=stats(t)[:, Q:], in_=sums[n][:], axis=AX.X, op=ALU.add)
+        def clamp(t):
+            cols = slice(0, 2 * Q if t in crosswise else Q)
+            excess[t] = work.tile([P, 2 * Q], F32, name="excess")
+            nc.scalar.activation(out=excess[t][:, cols], in_=sumsq[t][:, cols], func=ACT.Relu, bias=-EPS * EPS)
 
-        def clamp(t, cols):
-            small[t] = work.tile([P, 2 * Q], F32, name="excess")
-            nc.scalar.activation(out=small[t][:, cols], in_=sumsq[t][:, cols], func=ACT.Relu, bias=-EPS * EPS)
-
-        def root(t, cols):
-            quarters[t] = work.tile([P, 2 * Q], F32, name="quarter", bufs=8)
-            factor = 1.0 if KINDS[t] == "q" else 16.0
+        def weigh(t):
+            weights[t] = work.tile([P, 2 * Q], F32, name="weights", bufs=8)
+            factor = 1.0 if t in SENSE_STEPS else float(L * L)
             nc.scalar.activation(
-                out=quarters[t][:, 0:Q], in_=small[t][:, 0:Q], func=ACT.Abs_reciprocal_sqrt, scale=factor, bias=factor * EPS * EPS
+                out=weights[t][:, 0:Q], in_=excess[t][:, 0:Q], func=ACT.Abs_reciprocal_sqrt, scale=factor, bias=factor * EPS * EPS
             )
-            if cols.stop > Q:
+            if t in crosswise:
                 totals[t] = work.tile([P, 1], F32, name="total")
                 nc.scalar.activation(
-                    out=quarters[t][:, Q:],
-                    in_=small[t][:, Q:],
+                    out=weights[t][:, Q:],
+                    in_=excess[t][:, Q:],
                     func=ACT.Abs_reciprocal_sqrt,
-                    scale=16.0,
-                    bias=16.0 * EPS * EPS,
+                    scale=float(L * L),
+                    bias=L * L * EPS * EPS,
                     accum_out=totals[t][:],
                 )
 
-        def invert(t, cols):
-            j, h = once[t]
-            if KINDS[t] in "Zq":
-                for i in range(Q):
-                    if t < VSCALE:
-                        nc.vector.tensor_scalar(out=ys[t][:, i, :], in0=ys[t][:, i, :], scalar1=quarters[t][:, i : i + 1], scalar2=None, op0=ALU.mult)
-                    elif KINDS[t] == "Z" or WHO[h][i] == "G":
-                        pool_scale(t, i)
-                    if i == 0:
-                        finish()
-            if KINDS[t] == "Z":
-                if t >= MERGE:
-                    nc.gpsimd.tensor_tensor(out=ys[t][:, 0:2, :], in0=ys[t][:, 0:2, :], in1=ys[t][:, 2:4, :], op=ALU.add)
-                else:
-                    for i in range(2):
-                        nc.gpsimd.tensor_tensor(out=ys[t][:, i, :], in0=ys[t][:, i, :], in1=ys[t][:, i + 2, :], op=ALU.add)
-                pending.append(t)
-                if not DEFER or KINDS[t + 1] == "q" and WHO[once[t + 1][1]][0] != "G":
-                    finish()
 
-        def finish():
-            while pending:
-                t = pending.pop()
-                nc.gpsimd.tensor_tensor(out=ys[t][:, 0, :], in0=ys[t][:, 0, :], in1=ys[t][:, 1, :], op=ALU.add)
+        def scale(t, i, engine):
+            tile, weight = biased[t][:, i, :], weights[t][:, i : i + 1]
+            if engine == "gpsimd":
+                nc.gpsimd.tensor_scalar(out=tile, in0=tile, scalar1=weight, scalar2=0.0, op0=ALU.mult, op1=ALU.add)
+                return
+            if engine == "vector":
+                nc.vector.tensor_scalar(out=tile, in0=tile, scalar1=weight, scalar2=None, op0=ALU.mult)
+            else:
+                nc.scalar.activation(out=tile, in_=tile, func=ACT.Copy, scale=weight)
+            nc.sync.dma_start(out=out_0[direct[t][1], i * P : (i + 1) * P, :], in_=tile)
+
+        def pool_add(t, i, k):
+            nc.gpsimd.tensor_tensor(out=biased[t][:, i, :], in0=biased[t][:, i, :], in1=biased[t][:, k, :], op=ALU.add)
+
+        def pool_work(t):
+            j, h = direct[t]
+            for i in range(Q):
+                if j is not None or scaler(h, i) == "gpsimd":
+                    scale(t, i, "gpsimd")
+                if i == 0 and last_add:
+                    pool_add(last_add.pop(), 0, 1)
+            if j is not None:
+                pool_add(t, 0, 2)
+                pool_add(t, 1, 3)
+                next_block, next_head = direct[t + 1]
+                if next_block is None and scaler(next_head, 0) != "gpsimd":
+                    pool_add(t, 0, 1)
+                else:
+                    last_add.append(t)
 
         def pool_store(t):
-            j, h = once[t]
-            if j is None:
-                for i in [i for i in range(Q) if WHO[h][i] == "G"]:
-                    nc.sync.dma_start(out=out_0[h, i * P : (i + 1) * P, :], in_=ys[t][:, i, :])
+            j, h = direct[t]
+            if j is not None:
+                nc.sync.dma_start(out=out_1[h, j * P : (j + 1) * P, :], in_=biased[t][:, 0, :])
+            for i in range(Q):
+                if j is None and scaler(h, i) == "gpsimd":
+                    nc.sync.dma_start(out=out_0[h, i * P : (i + 1) * P, :], in_=biased[t][:, i, :])
+
+
+        def start_sum(t):
+            sums[t] = work.tile([P, E], F32, name="sum", bufs=6)
+            if t in VECTOR_START_STEPS:
+                nc.vector.tensor_scalar(out=sums[t][:], in0=banks["bias", t][:], scalar1=totals[t][:], scalar2=None, op0=ALU.mult)
             else:
-                nc.sync.dma_start(out=out_1[h, j * P : (j + 1) * P, :], in_=ys[t][:, 0, :])
+                nc.scalar.activation(out=sums[t][:], in_=bias_wide[crosswise[t][1]], func=ACT.Copy, scale=totals[t][:])
 
-        def scalar_scale(t, i, on_vector):
-            if on_vector == "G":
-                pool_scale(t, i)
-            elif on_vector == "V":
-                nc.vector.tensor_scalar(out=ys[t][:, i, :], in0=ys[t][:, i, :], scalar1=quarters[t][:, i : i + 1], scalar2=None, op0=ALU.mult)
-            else:
-                nc.scalar.activation(out=ys[t][:, i, :], in_=ys[t][:, i, :], func=ACT.Copy, scale=quarters[t][:, i : i + 1])
-            nc.sync.dma_start(out=out_0[once[t][1], i * P : (i + 1) * P, :], in_=ys[t][:, i, :])
-
-        def total_weight(t):
-            first = again[t][1]
-            totals[t] = work.tile([P, 1], F32, name="total")
-            nc.vector.tensor_reduce(out=totals[t][:], in_=quarters[t][:, first : first + Q], axis=AX.X, op=ALU.add)
-
-        def bias_share(t):
-            accs[t] = work.tile([P, E], F32, name="acc", bufs=6)
-            nc.scalar.activation(out=accs[t][:], in_=bias_all[again[t][0][1]], func=ACT.Copy, scale=totals[t][:])
-
-        def add_word(t, i):
-            (j, h), first = again[t]
+        def add_word(t, l):
+            first = t - LAG
+            j, h = crosswise[first]
             nc.vector.scalar_tensor_tensor(
-                out=accs[t][:], in0=banks["b", t, i][:], scalar=quarters[t][:, first + i : first + i + 1], in1=accs[t][:], op0=ALU.mult, op1=ALU.add
+                out=sums[first][:],
+                in0=banks["s", t, l][:],
+                scalar=weights[first][:, Q + l : Q + l + 1],
+                in1=sums[first][:],
+                op0=ALU.mult,
+                op1=ALU.add,
             )
-            if i == Q - 1:
-                nc.sync.dma_start(out=out_1[h, j * P : (j + 1) * P, :], in_=accs[t][:])
+            if l == L - 1:
+                nc.sync.dma_start(out=out_1[h, j * P : (j + 1) * P, :], in_=sums[first][:])
 
-        def pool_scale(t, i):
-            j, h = once[t]
-            nc.gpsimd.tensor_scalar(
-                out=ys[t][:, i, :], in0=ys[t][:, i, :], scalar1=quarters[t][:, i : i + 1], scalar2=0.0, op0=ALU.mult, op1=ALU.add
-            )
+        def run(calls):
+            for call, *args in calls:
+                call(*args)
 
-        turn(batches[0])
-        copy_out(False)
-        copy_out(True)
-        quantise(batches[0])
-        turn(batches[1])
-        for half in range(2):
-            copy_out(half == 1)
-            quantise(batches[1], half, 2)
+        turn(units[0])
+        copy_out("scalar")
+        copy_out("vector")
+        quantise(units[0])
+        turn(units[1])
         spread_bias(0)
+        copy_out("scalar")
+        quantise(units[1], slice(0, 2 * P))
+        copy_out("vector")
         spread_copy()
-        turn(batches[2])
+        quantise(units[1], slice(2 * P, Q * P))
 
-        for t in range(n_steps + 1):
-            plain = once[t] if t < n_steps else None
-            front, middle, back = t in crosswise, t - 1 in crosswise, t - LAG in again
-            last = t == n_steps - 1 and LASTORD
-            fresh = ready[t - 1]
-            cols = slice(0, 2 * Q if middle else Q)
-            if middle:
-                fold_sum(t - 1, t - 1)
-            order = (("p", 0), ("b", 0), ("f", 0), ("f", 1), ("p", 1), ("f", 2), ("b", 1), ("f", 3), ("p", 2), ("b", 2), ("p", 3), ("b", 3))
-            if last:
-                order = (("p", 0), ("p", 1), ("b", 0), ("p", 2), ("b", 1), ("p", 3), ("b", 2), ("b", 3))
-            for kind, i in order:
-                if kind == "p" and plain:
-                    mm(("p", t, i), ("F", plain[0]), i, ("W", plain[1]))
-                if kind == "b" and back:
-                    mm(("b", t - LAG, i), ("F", again[t - LAG][0][0]), i, ("W", again[t - LAG][0][1]))
-                if kind == "f" and front:
-                    mm(("f", t, i), ("W", crosswise[t][1]), i, ("F", crosswise[t][0]))
-            if t == 0:
-                turn(batches[3])
-                bias_columns_turn()
-            on_vector = min(len(turned), VCOPY[t] if t < len(VCOPY) else VLATE)
-            first_half = [(copy_out, (False,)) for n in range(len(turned) - on_vector)]
-            first_half += [(turned_squares, (t, i)) for i in range(Q) if front]
-            if 0 < t < n_steps:
-                first_half.insert(1, (clamp, (t - 1, cols)))
-                first_half.insert(3, (root, (t - 1, cols)))
-            for call, args in first_half:
-                call(*args)
-            vec = [(copy_out, (True,)) for n in range(on_vector)]
-            rows = [(add_bias if kind == "p" else add_word, (t if kind == "p" else t - LAG, i)) for kind, i in order if kind == "p" and plain or kind == "b" and back]
-            if t == 0:
-                vec = rows[:2] + [(quantise, (fresh[0],))] + rows[2:3] + vec + rows[3:] + [(quantise, (fresh[1],)), (bias_columns_copy, ())]
-            else:
-                vec = vec[:1] + rows[:1] + vec[1:] + rows[1:]
-                vec.insert((INV - middle) if plain else 1, (invert, (t - 1, cols)))
-                if fresh:
-                    vec.insert(len(vec) - QPOS, (quantise, (fresh[0],)))
-            if t == SPREAD_AT + 1:
-                vec = [(spread_copy, ())] + vec[:2] + [(spread_copy, ())] + vec[2:]
-            late = [i for i in range(Q) if t > 0 and KINDS[t - 1] == "q" and WHO[once[t - 1][1]][i] == "S"]
-            if not plain:
-                for n, i in enumerate([i for i in range(Q) if WHO[-1][i] == "V"]):
-                    vec.insert(3 + 2 * n, (scalar_scale, (t - 1, i, "V")))
-                for n, i in enumerate(late):
-                    vec.insert(2, (scalar_scale, (t - 1, i, "S")))
-            for call, args in vec:
-                call(*args)
-            for batch in ready[t]:
-                turn(batch)
-            if t == SPREAD_AT:
-                spread_bias(1)
-                spread_bias(2)
-            if front:
-                fold(t, range(Q))
-            second_half = [(row_squares, (t, i)) for i in range(Q) if plain]
-            if t - 1 in again:
-                second_half.insert(SHARE_AT + 1, (bias_share, (t - 1,)))
-            if t == n_steps - 1:
-                second_half += [(clamp, (t, slice(0, Q))), (root, (t, slice(0, Q)))]
-            if plain:
-                for n, i in enumerate(late[::-1]):
-                    second_half.insert(len(second_half) - 2 * n - LATE_OFF, (scalar_scale, (t - 1, i, "S")))
-            for call, args in second_half:
-                call(*args)
-            if t - 1 - GLAG >= 0 and KINDS[t - 1 - GLAG] in "Zq":
-                pool_store(t - 1 - GLAG)
-        for t in range(n_steps - GLAG, n_steps):
-            if KINDS[t] in "Zq":
-                pool_store(t)
+        products(0, [("d", 0), ("d", 1)])
+        turn(units[2])
+        products(0, [("d", 2), ("d", 3)])
+        turn(units[3], (0,))
+        for i in range(2):
+            add_bias(0, i)
+            row_squares(0, i)
+        copy_out("vector")
+        copy_out("scalar")
+        add_bias(0, 2)
+        row_squares(0, 2)
+        add_bias(0, 3)
+        quantise(units[2])
+        turn(units[3], (1,))
+        copy_out("scalar")
+        row_squares(0, 3)
+        copy_out("vector")
+        spread_bias(1)
+        bias_turned = psum.tile([P, Q, P], BF16, name="bank")
+        for c in range(Q):
+            nc.tensor.transpose(bias_turned[:, c, :], bias_rows[:, c * P : (c + 1) * P], ident_bf[:])
+        turn(units[4], (0,))
+        spread_bias(2)
+        turn(units[4], (1,))
+        clamp(0)
+        quantise(units[3])
+        nc.vector.tensor_copy(out=bias_col[:], in_=bias_turned[:, :, 0:HEADS])
+        copy_out("scalar")
+        weigh(0)
+        spread_copy()
+
+        product_order = [("d", 0), ("s", 0), ("f", 0), ("f", 1), ("d", 1), ("f", 2), ("s", 1), ("f", 3)]
+        product_order += [(kind, i) for i in (2, 3) for kind in "ds"]
+
+        for t in range(1, STEPS + 1):
+            there = {"d": t < STEPS, "f": t in crosswise, "s": t - LAG in crosswise}
+            order = [(kind, i) for kind, i in product_order if there[kind]]
+            before = t - 1
+
+            held = (3 if there["s"] else 1) if t in turned_in else 0
+            if before in crosswise:
+                nc.vector.tensor_reduce(out=sumsq[before][:, Q:], in_=folded[before][:], axis=AX.X, op=ALU.add)
+            products(t, order[: len(order) - held])
+
+            first_half = [(column_squares, t, c) for c in range(Q) if there["f"]]
+            if 1 < t < STEPS:
+                first_half.insert(1, (clamp, before))
+                first_half.insert(3, (weigh, before))
+            run(first_half)
+            pool_work(before)
+
+            reads = [(add_bias if kind == "d" else add_word, t, i) for kind, i in order if kind != "f"]
+            sense_tiles = [(scale, before, i, scaler(direct[before][1], i)) for i in range(Q) if before in SENSE_STEPS]
+            on_scalar = [call for call in sense_tiles if call[-1] == "scalar"]
+            if t == STEPS:
+                for n, call in enumerate([call for call in sense_tiles if call[-1] == "vector"]):
+                    reads.insert(2 + 2 * n, call)
+                for call in on_scalar:
+                    reads.insert(1, call)
+            early, rest = reads[: len(reads) - held], reads[len(reads) - held :]
+            if before in turned_in:
+                early.insert(1, (copy_out, "vector"))
+                early.insert(5, (quantise, turned_in[before]))
+            if t == 1:
+                early.insert(2, (spread_copy,))
+            run(early)
+            if t in turned_in:
+                turn(turned_in[t])
+            products(t, order[len(order) - held :])
+            if before in VECTOR_START_STEPS:
+                banks["bias", before] = psum.tile([P, E], F32, name="bank")
+                bias_on_all_partitions(banks["bias", before][:], crosswise[before][1])
+                rest.append((start_sum, before))
+            if t in turned_in and not there["s"]:
+                rest.insert(1, (copy_out, "vector"))
+            run(rest)
+            if there["f"]:
+                fold(t)
+
+            second_half = [(row_squares, t, i) for i in range(Q) if there["d"]]
+            if before in crosswise and before not in VECTOR_START_STEPS:
+                second_half.insert(2, (start_sum, before))
+            if t in turned_in and there["s"]:
+                second_half.insert(1, (copy_out, "scalar"))
+            if t == STEPS - 1:
+                second_half += [(clamp, t), (weigh, t)]
+            if there["d"]:
+                for n, call in enumerate(on_scalar[::-1]):
+                    second_half.insert(len(second_half) - 1 - 2 * n, call)
+            run(second_half)
+
+            if t >= 2:
+                pool_store(t - 2)

from contextlib import ExitStack

import concourse.mybir as mybir
from concourse.masks import make_identity

N, L, H, E, HEADS = 512, 4, 512, 512, 6
EPS = 1e-12
FLOPS = 2 * HEADS * N * (L + 1) * H * E

F32 = mybir.dt.float32
BF16 = mybir.dt.bfloat16
U32 = mybir.dt.uint32
U8 = mybir.dt.uint8
FORMAT = {"W": mybir.dt.float8_e4m3fn_x4, "X": mybir.dt.float8_e5m2_x4}
ALU = mybir.AluOpType
ACT = mybir.ActivationFunctionType
AX = mybir.AxisListType

P = 128
Q = 4
BANKS = 8

DIRECT_MEANS = 10
STEPS = DIRECT_MEANS + HEADS
FIRST_SENSE_STEP = 6
SENSE_STEPS = list(range(FIRST_SENSE_STEP, STEPS, 2)) + [STEPS - 1]
LAG = 2
POOL_SENSE_TILES = 15
VECTOR_START_STEPS = range(8, STEPS - LAG, 2)


def tile_biencodermodel_pa_kernel(tc, feature, aspect_v, W, b, out_0, out_1):
    nc = tc.nc
    with ExitStack() as ctx:
        keep = ctx.enter_context(tc.tile_pool(name="keep", bufs=1))
        work = ctx.enter_context(tc.tile_pool(name="work", bufs=2))
        psum = ctx.enter_context(tc.psum_pool(name="psum", bufs=BANKS))
        ctx.enter_context(tc.manual_schedule())

        units = [("W", 0), ("X", 0), ("X", 1), ("W", 1), ("X", 2), ("X", 3), ("W", 2), ("X", None)]
        units += [("W", h) for h in range(3, HEADS)]
        sources = {("W", h): W[h].rearrange("(c p) k -> p c k", p=P) for h in range(HEADS)}
        sources.update({("X", j): feature[j * P : (j + 1) * P] for j in range(Q)})
        sources["X", None] = aspect_v.rearrange("(j p) k -> p j k", p=P)

        means = sorted(
            [(j, h) for j in range(Q) for h in range(HEADS)],
            key=lambda job: max(units.index(("X", job[0])), units.index(("W", job[1]))),
        )
        direct, crosswise = [], {}
        for t in range(STEPS):
            direct.append((None, SENSE_STEPS.index(t)) if t in SENSE_STEPS else means.pop(0))
            if 1 <= t <= STEPS - LAG:
                crosswise[t] = means.pop(0)
        assert not means
        turned_in = {t: units[t + 4] for t in range(len(units) - 4)}

        def scaler(h, i):
            if Q * h + i < POOL_SENSE_TILES:
                return "gpsimd"
            return "vector" if h == HEADS - 1 and i % 2 == 1 else "scalar"

        bias_rows = keep.tile([P, E], BF16, name="bias_rows")
        nc.vector.memset(bias_rows[:], 0.0)
        nc.scalar.dma_start(out=bias_rows[0:HEADS, :], in_=b)

        raw = {}
        for unit in units:
            raw[unit] = keep.tile([P, Q, H], BF16, name="raw_%s%s" % unit)
            for part in (slice(0, 2), slice(2, Q)) if unit in units[:2] else (slice(0, Q),):
                nc.sync.dma_start(out=raw[unit][:, part, :], in_=sources[unit][:, part, :])

        ident = keep.tile([P, P], F32, name="ident")
        make_identity(nc, ident[:])
        ident_bf = keep.tile([P, P], BF16, name="ident_bf")
        make_identity(nc, ident_bf[:])
        bias_col = keep.tile([P, Q, HEADS], F32, name="bias_col")

        grouped, codes, scales, bias_wide = {}, {}, {}, {}
        banks, squares, folded, biased, sums = {}, {}, {}, {}, {}
        sumsq, excess, weights, totals = {}, {}, {}, {}
        to_copy, to_spread, last_add = [], [], []


        def turn(unit, halves=(0, 1)):
            if halves[0] == 0:
                grouped[unit] = work.tile([P, Q * P * 4], BF16, name="grouped", align_bytes=64, bufs=3)
            pairs = grouped[unit][:].bitcast(F32).rearrange("p (i r u) -> p i r u", r=P, u=2)
            for half in halves:
                bank = psum.tile([P, 2, 2, P], F32, name="bank")
                for i in range(2):
                    words = raw[unit][:, 2 * half + i, :].bitcast(F32)
                    for u in range(2):
                        nc.tensor.transpose(bank[:, i, u, :], words[:, u::2], ident[:])
                to_copy.append((pairs[:, 2 * half : 2 * half + 2], bank[:].rearrange("p i u r -> p i r u")))

        def copy_out(engine):
            dst, src = to_copy.pop(0)
            if engine == "vector":
                nc.vector.tensor_copy(out=dst, in_=src)
            else:
                nc.scalar.copy(out=dst, in_=src)

        def quantise(unit, rows=slice(0, Q * P)):
            if rows.start == 0:
                codes[unit] = keep.tile([P, Q * P], U32, name="codes_%s%s" % unit, align_bytes=64)
                scales[unit] = keep.tile([P, Q * P], U8, name="scales_%s%s" % unit, align_bytes=64)
            nc.vector.quantize_mx(
                out=codes[unit][:, rows].bitcast(FORMAT[unit[0]]),
                scales=scales[unit][:, rows],
                in_=grouped[unit][:, 4 * rows.start : 4 * rows.stop],
            )


        def bias_on_all_partitions(out, h):
            nc.tensor.matmul(
                out=out, lhsT=ident_bf[:, h : h + 1].to_broadcast([P, P]), rhs=bias_rows[:], start=True, stop=True
            )

        def spread_bias(pair):
            bank = psum.tile([P, 2, E], BF16, name="bank")
            both = keep.tile([P, 2, E], BF16, name="bias_pair%d" % pair)
            for n in range(2):
                bias_on_all_partitions(bank[:, n, :], 2 * pair + n)
                bias_wide[2 * pair + n] = both[:, n, :]
            to_spread.append((both, bank))

        def spread_copy():
            both, bank = to_spread.pop(0)
            nc.vector.tensor_copy(out=both[:], in_=bank[:])


        def products(t, order):
            for kind, i in order:
                j, h = {"d": direct[t : t + 1], "f": [crosswise.get(t)], "s": [crosswise.get(t - LAG)]}[kind][0]
                stationary, moving = (("W", h), ("X", j)) if kind == "f" else (("X", j), ("W", h))
                cols = slice(i * P, (i + 1) * P)
                banks[kind, t, i] = psum.tile([P, E], F32, name="bank")
                nc.tensor.matmul_mx(
                    out=banks[kind, t, i][:],
                    lhsT=codes[stationary][:, cols].bitcast(FORMAT[stationary[0]]),
                    lhsT_scale=scales[stationary][:, cols],
                    rhs=codes[moving][:].bitcast(FORMAT[moving[0]]),
                    rhs_scale=scales[moving][:],
                    start=True,
                    stop=True,
                )


        def add_bias(t, i):
            if i == 0:
                biased[t] = work.tile([P, Q, E], F32, name="biased", bufs=6)
            nc.vector.tensor_tensor(out=biased[t][:, i, :], in0=banks["d", t, i][:], in1=bias_wide[direct[t][1]], op=ALU.add)

        def row_squares(t, i):
            if i == 0:
                sumsq[t] = work.tile([P, 2 * Q], F32, name="sumsq", bufs=3)
            unread = work.tile([P, E], BF16, name="unread")
            nc.scalar.activation(out=unread[:], in_=biased[t][:, i, :], func=ACT.Square, accum_out=sumsq[t][:, i : i + 1])

        def column_squares(t, c):
            if c == 0:
                squares[t] = work.tile([P, Q, E], F32, name="squares")
            h = crosswise[t][1]
            nc.scalar.activation(out=squares[t][:, c, :], in_=banks["f", t, c][:], func=ACT.Square, bias=bias_col[:, c, h : h + 1])

        def fold(t):
            folded[t] = psum.tile([P, Q, P], F32, name="bank")
            for l in range(L):
                for c in range(Q):
                    nc.tensor.matmul(
                        out=folded[t][:, l, :],
                        lhsT=squares[t][:, c, l * P : (l + 1) * P],
                        rhs=ident[:],
                        start=(c == 0),
                        stop=(c == Q - 1),
                        is_transpose=True,
                    )

        def clamp(t):
            cols = slice(0, 2 * Q if t in crosswise else Q)
            excess[t] = work.tile([P, 2 * Q], F32, name="excess")
            nc.scalar.activation(out=excess[t][:, cols], in_=sumsq[t][:, cols], func=ACT.Relu, bias=-EPS * EPS)

        def weigh(t):
            weights[t] = work.tile([P, 2 * Q], F32, name="weights", bufs=8)
            factor = 1.0 if t in SENSE_STEPS else float(L * L)
            nc.scalar.activation(
                out=weights[t][:, 0:Q], in_=excess[t][:, 0:Q], func=ACT.Abs_reciprocal_sqrt, scale=factor, bias=factor * EPS * EPS
            )
            if t in crosswise:
                totals[t] = work.tile([P, 1], F32, name="total")
                nc.scalar.activation(
                    out=weights[t][:, Q:],
                    in_=excess[t][:, Q:],
                    func=ACT.Abs_reciprocal_sqrt,
                    scale=float(L * L),
                    bias=L * L * EPS * EPS,
                    accum_out=totals[t][:],
                )


        def scale(t, i, engine):
            tile, weight = biased[t][:, i, :], weights[t][:, i : i + 1]
            if engine == "gpsimd":
                nc.gpsimd.tensor_scalar(out=tile, in0=tile, scalar1=weight, scalar2=0.0, op0=ALU.mult, op1=ALU.add)
                return
            if engine == "vector":
                nc.vector.tensor_scalar(out=tile, in0=tile, scalar1=weight, scalar2=None, op0=ALU.mult)
            else:
                nc.scalar.activation(out=tile, in_=tile, func=ACT.Copy, scale=weight)
            nc.sync.dma_start(out=out_0[direct[t][1], i * P : (i + 1) * P, :], in_=tile)

        def pool_add(t, i, k):
            nc.gpsimd.tensor_tensor(out=biased[t][:, i, :], in0=biased[t][:, i, :], in1=biased[t][:, k, :], op=ALU.add)

        def pool_work(t):
            j, h = direct[t]
            for i in range(Q):
                if j is not None or scaler(h, i) == "gpsimd":
                    scale(t, i, "gpsimd")
                if i == 0 and last_add:
                    pool_add(last_add.pop(), 0, 1)
            if j is not None:
                pool_add(t, 0, 2)
                pool_add(t, 1, 3)
                next_block, next_head = direct[t + 1]
                if next_block is None and scaler(next_head, 0) != "gpsimd":
                    pool_add(t, 0, 1)
                else:
                    last_add.append(t)

        def pool_store(t):
            j, h = direct[t]
            if j is not None:
                nc.sync.dma_start(out=out_1[h, j * P : (j + 1) * P, :], in_=biased[t][:, 0, :])
            for i in range(Q):
                if j is None and scaler(h, i) == "gpsimd":
                    nc.sync.dma_start(out=out_0[h, i * P : (i + 1) * P, :], in_=biased[t][:, i, :])


        def start_sum(t):
            sums[t] = work.tile([P, E], F32, name="sum", bufs=6)
            if t in VECTOR_START_STEPS:
                nc.vector.tensor_scalar(out=sums[t][:], in0=banks["bias", t][:], scalar1=totals[t][:], scalar2=None, op0=ALU.mult)
            else:
                nc.scalar.activation(out=sums[t][:], in_=bias_wide[crosswise[t][1]], func=ACT.Copy, scale=totals[t][:])

        def add_word(t, l):
            first = t - LAG
            j, h = crosswise[first]
            nc.vector.scalar_tensor_tensor(
                out=sums[first][:],
                in0=banks["s", t, l][:],
                scalar=weights[first][:, Q + l : Q + l + 1],
                in1=sums[first][:],
                op0=ALU.mult,
                op1=ALU.add,
            )
            if l == L - 1:
                nc.sync.dma_start(out=out_1[h, j * P : (j + 1) * P, :], in_=sums[first][:])

        def run(calls):
            for call, *args in calls:
                call(*args)

        turn(units[0])
        copy_out("scalar")
        copy_out("vector")
        quantise(units[0])
        turn(units[1])
        spread_bias(0)
        copy_out("scalar")
        quantise(units[1], slice(0, 2 * P))
        copy_out("vector")
        spread_copy()
        quantise(units[1], slice(2 * P, Q * P))

        products(0, [("d", 0), ("d", 1)])
        turn(units[2])
        products(0, [("d", 2), ("d", 3)])
        turn(units[3], (0,))
        for i in range(2):
            add_bias(0, i)
            row_squares(0, i)
        copy_out("vector")
        copy_out("scalar")
        add_bias(0, 2)
        row_squares(0, 2)
        add_bias(0, 3)
        quantise(units[2])
        turn(units[3], (1,))
        copy_out("scalar")
        row_squares(0, 3)
        copy_out("vector")
        spread_bias(1)
        bias_turned = psum.tile([P, Q, P], BF16, name="bank")
        for c in range(Q):
            nc.tensor.transpose(bias_turned[:, c, :], bias_rows[:, c * P : (c + 1) * P], ident_bf[:])
        turn(units[4], (0,))
        spread_bias(2)
        turn(units[4], (1,))
        clamp(0)
        quantise(units[3])
        nc.vector.tensor_copy(out=bias_col[:], in_=bias_turned[:, :, 0:HEADS])
        copy_out("scalar")
        weigh(0)
        spread_copy()

        product_order = [("d", 0), ("s", 0), ("f", 0), ("f", 1), ("d", 1), ("f", 2), ("s", 1), ("f", 3)]
        product_order += [(kind, i) for i in (2, 3) for kind in "ds"]

        for t in range(1, STEPS + 1):
            there = {"d": t < STEPS, "f": t in crosswise, "s": t - LAG in crosswise}
            order = [(kind, i) for kind, i in product_order if there[kind]]
            before = t - 1

            held = (3 if there["s"] else 1) if t in turned_in else 0
            if before in crosswise:
                nc.vector.tensor_reduce(out=sumsq[before][:, Q:], in_=folded[before][:], axis=AX.X, op=ALU.add)
            products(t, order[: len(order) - held])

            first_half = [(column_squares, t, c) for c in range(Q) if there["f"]]
            if 1 < t < STEPS:
                first_half.insert(1, (clamp, before))
                first_half.insert(3, (weigh, before))
            run(first_half)
            pool_work(before)

            reads = [(add_bias if kind == "d" else add_word, t, i) for kind, i in order if kind != "f"]
            sense_tiles = [(scale, before, i, scaler(direct[before][1], i)) for i in range(Q) if before in SENSE_STEPS]
            on_scalar = [call for call in sense_tiles if call[-1] == "scalar"]
            if t == STEPS:
                for n, call in enumerate([call for call in sense_tiles if call[-1] == "vector"]):
                    reads.insert(2 + 2 * n, call)
                for call in on_scalar:
                    reads.insert(1, call)
            early, rest = reads[: len(reads) - held], reads[len(reads) - held :]
            if before in turned_in:
                early.insert(1, (copy_out, "vector"))
                early.insert(5, (quantise, turned_in[before]))
            if t == 1:
                early.insert(2, (spread_copy,))
            run(early)
            if t in turned_in:
                turn(turned_in[t])
            products(t, order[len(order) - held :])
            if before in VECTOR_START_STEPS:
                banks["bias", before] = psum.tile([P, E], F32, name="bank")
                bias_on_all_partitions(banks["bias", before][:], crosswise[before][1])
                rest.append((start_sum, before))
            if t in turned_in and not there["s"]:
                rest.insert(1, (copy_out, "vector"))
            run(rest)
            if there["f"]:
                fold(t)

            second_half = [(row_squares, t, i) for i in range(Q) if there["d"]]
            if before in crosswise and before not in VECTOR_START_STEPS:
                second_half.insert(2, (start_sum, before))
            if t in turned_in and there["s"]:
                second_half.insert(1, (copy_out, "scalar"))
            if t == STEPS - 1:
                second_half += [(clamp, t), (weigh, t)]
            if there["d"]:
                for n, call in enumerate(on_scalar[::-1]):
                    second_half.insert(len(second_half) - 1 - 2 * n, call)
            run(second_half)

            if t >= 2:
                pool_store(t - 2)
